import numpy as np
import ml_dtypes


def mxq(x, axis, fmt="e4m3"):
    dtype, down = {"e4m3": (ml_dtypes.float8_e4m3fn, 7), "e5m2": (ml_dtypes.float8_e5m2, 14)}[fmt]
    v = np.moveaxis(np.asarray(x, np.float32).astype(ml_dtypes.bfloat16).astype(np.float64), axis, -1)
    blocks = v.reshape(v.shape[:-1] + (-1, 32))
    amax = np.abs(blocks).max(-1, keepdims=True)
    byte = np.maximum(np.where(amax > 0, np.frexp(amax)[1] - 1 + 127, 0) - down, 1)
    scale = np.exp2(byte - 127.0)
    codes = (blocks / scale).astype(np.float32).astype(dtype).astype(np.float64)
    return np.moveaxis((codes * scale).reshape(v.shape), -1, axis)


WIDE = False


def mx_kscale(k):
    if not WIDE:
        return np.ones(k)
    levels = np.array([30, -30])
    if k % 512:
        return np.exp2(np.random.permutation(np.resize(levels, k // 32))).repeat(32)
    a = np.empty((k // 512, 16))
    for p in range(k // 512):
        a[p, :8] = np.random.permutation(np.resize(levels, 8))
        for g in range(8):
            far = levels[np.abs(levels - a[p, g]) >= 10]
            a[p, g + 8] = far[np.random.randint(len(far))]
    return np.exp2(a.ravel()).repeat(32)


BF16 = ml_dtypes.bfloat16


def bf(x):
    return np.asarray(x, np.float32).astype(BF16)


def f64(x):
    return np.asarray(x).astype(np.float64)


E2M1 = np.array([0.0, 0.5, 1.0, 1.5, 2.0, 3.0, 4.0, 6.0, -0.0, -0.5, -1.0, -1.5, -2.0, -3.0, -4.0, -6.0])


def pack_weight(w, fmt):
    k, n = w.shape
    w = f64(bf(w)).reshape(k // 32, 32, n)
    amax = np.abs(w).max(1)
    if fmt == "e4m3":
        byte = np.frexp(amax)[1] - 1 + 127 - 7
    else:
        mant, ex = np.frexp(amax / 6.0)
        byte = np.where(mant > 0.5, ex, ex - 1) + 127
    byte = np.clip(np.where(amax > 0, byte, 1), 1, 254)
    scaled = (w * np.exp2(127.0 - byte)[:, None, :]).reshape(k, n).astype(np.float32)
    by_word = np.ascontiguousarray(scaled.reshape(k // 512, 128, 4, n).transpose(0, 1, 3, 2))
    if fmt == "e4m3":
        words = by_word.astype(ml_dtypes.float8_e4m3fn).view(np.uint8)
    else:
        c = by_word.astype(ml_dtypes.float4_e2m1fn).view(np.uint8) & 0xF
        words = c[..., 0::2] | (c[..., 1::2] << 4)
    return np.ascontiguousarray(words), np.ascontiguousarray(byte.astype(np.uint8).reshape(k // 512, 16, n))


def unpack_weight(words, scales, fmt):
    g, p, n, _ = words.shape
    if fmt == "e4m3":
        vals = np.ascontiguousarray(words).view(ml_dtypes.float8_e4m3fn).astype(np.float64)
    else:
        nib = np.empty((g, p, n, 4), np.uint8)
        nib[..., 0::2] = words & 0xF
        nib[..., 1::2] = words >> 4
        vals = E2M1[nib]
    vals = vals * np.repeat(np.exp2(scales.astype(np.float64) - 127.0), 8, axis=1)[..., None]
    return vals.transpose(0, 1, 3, 2).reshape(g * 512, n)

def pack4(w):
    words, scales = pack_weight(w, "e2m1")
    return words.reshape(words.shape[0], 128, -1), scales


def unpack4(words, scales):
    return unpack_weight(words.reshape(words.shape[0], 128, -1, 2), scales, "e2m1")


B, S, D = 1, 512, 2048
ROPE_BASE = 10000.0


def rope_tables():
    inv_freq = 1.0 / ROPE_BASE ** (np.arange(0, D, 2) / D)
    freqs = np.outer(np.arange(S), inv_freq)
    emb = np.concatenate([freqs, freqs], axis=-1)
    return np.cos(emb), np.sin(emb)


def rotate_half(u):
    u1, u2 = np.split(u, 2, axis=-1)
    return np.concatenate([-u2, u1], axis=-1)


def setup_inputs():
    s = mx_kscale(D)
    c, sn = rope_tables()
    w = 1.0 / np.sqrt(D)
    x = bf(np.random.standard_normal((B, S, D)) * s)
    wq = np.random.standard_normal((D, D)) * w / s[None, :]
    wk = np.random.standard_normal((D, D)) * w / s[None, :]
    wq_words, wq_scales = pack4(np.ascontiguousarray(wq.T))
    wk_words, wk_scales = pack4(np.ascontiguousarray(wk.T))
    return {"x": x,
            "cos": bf(c),
            "sin": bf(sn),
            "Wq_words": wq_words,
            "Wq_scales": wq_scales,
            "Wk_words": wk_words,
            "Wk_scales": wk_scales}


def reference(x, cos, sin, Wq_words, Wq_scales, Wk_words, Wk_scales):
    xq = mxq(f64(x), 2, "e5m2")
    q = xq @ unpack4(Wq_words, Wq_scales)
    k = xq @ unpack4(Wk_words, Wk_scales)
    c, sn = f64(cos), f64(sin)
    q_rot = q * c + rotate_half(q) * sn
    k_rot = k * c + rotate_half(k) * sn
    return q_rot, k_rot

@@ -1,0 +1,183 @@
+from contextlib import ExitStack
+
+import concourse.mybir as mybir
+from concourse.masks import make_identity
+
+S, D = 512, 2048
+FLOPS = 2 * 2 * S * D * D
+
+F32 = mybir.dt.float32
+BF16 = mybir.dt.bfloat16
+I32 = mybir.dt.int32
+U32 = mybir.dt.uint32
+U8 = mybir.dt.uint8
+E5M2X4 = mybir.dt.float8_e5m2_x4
+E2M1X4 = mybir.dt.float4_e2m1fn_x4
+MULT = mybir.AluOpType.mult
+ADD = mybir.AluOpType.add
+
+P = 128
+PASSES = 4
+K_HALF = D // 2
+N = 512
+ROT = D // 2
+TILES = S // P
+Q, K = 0, 1
+
+
+def tile_attention_pa_kernel(tc, x, cos, sin, Wq_words, Wq_scales, Wk_words, Wk_scales, out_0, out_1):
+    nc = tc.nc
+    w_words_hbm = (Wq_words, Wk_words)
+    w_scales_hbm = (Wq_scales, Wk_scales)
+    outs = (out_0, out_1)
+
+    with ExitStack() as ctx:
+        keep = ctx.enter_context(tc.tile_pool(name="keep", bufs=1))
+        stage = ctx.enter_context(tc.tile_pool(name="stage", bufs=3))
+        tr_psum = ctx.enter_context(tc.psum_pool(name="tr_psum", bufs=2))
+        mx_psum = ctx.enter_context(tc.psum_pool(name="mx_psum", bufs=6))
+        ctx.enter_context(tc.manual_schedule())
+
+        x_raw, x_codes, x_scales = {}, {}, {}
+        w_words, w_scales, planes = {}, {}, {}
+        cos_sb, sin_sb = {}, {}
+
+        def paired(rows, c):
+            return rows.rearrange("p (half n) -> p half n", half=2)[:, :, c * N:(c + 1) * N]
+
+        def zero_plane(m, col, width):
+            plane = keep.tile([P, PASSES, width], U8, name=f"plane_{m}_{col}", align_bytes=64)
+            nc.vector.memset(plane[:].rearrange("p g n -> p (g n)").bitcast(I32), 0)
+            planes[m, col] = plane
+            for c0 in range(col, col + width, N):
+                w_scales[m, c0] = plane[:, :, c0 - col:c0 - col + N]
+
+        def load_scales(m, col, width):
+            for r in range(4):
+                nc.sync.dma_start(
+                    out=planes[m, col][r:P:32, :, :].bitcast(I32),
+                    in_=w_scales_hbm[m][:, r:16:4, col:col + width].rearrange("g q n -> q g n").bitcast(I32),
+                )
+
+        def load_words(m, col):
+            words = keep.tile([P, PASSES, 2 * N], U8, name=f"words_{m}_{col}", align_bytes=64)
+            nc.sync.dma_start(
+                out=words[:].bitcast(I32),
+                in_=w_words_hbm[m][:, :, 2 * col:2 * (col + N)].rearrange("g p n -> p g n").bitcast(I32),
+            )
+            w_words[m, col] = words
+
+        def load_x(t):
+            for kh in range(2):
+                raw = keep.tile([P, K_HALF], BF16, name=f"x_{t}_{kh}", align_bytes=64)
+                nc.sync.dma_start(out=raw[:], in_=x[0, t * P:(t + 1) * P, kh * K_HALF:(kh + 1) * K_HALF])
+                x_raw[t, kh] = raw
+
+        def load_tables(t, c):
+            for name, table, tiles in (("cos", cos, cos_sb), ("sin", sin, sin_sb)):
+                tile = keep.tile([P, 2, N], BF16, name=f"{name}_{t}_{c}", align_bytes=64)
+                nc.sync.dma_start(out=tile[:], in_=paired(table[t * P:(t + 1) * P, :], c))
+                tiles[t, c] = tile
+
+        ident = keep.tile([P, P], F32, name="ident", align_bytes=64)
+        make_identity(nc, ident[:])
+
+        scale_runs = [(Q, 0, N), (Q, ROT, N), (K, 0, D), (Q, N, N), (Q, ROT + N, N)]
+        for run in scale_runs:
+            zero_plane(*run)
+
+        load_x(0)
+        load_scales(*scale_runs[0])
+        load_words(Q, 0)
+        load_x(1)
+        load_tables(0, 0)
+        load_scales(*scale_runs[1])
+        load_words(Q, ROT)
+        load_x(2)
+        load_tables(1, 0)
+        load_x(3)
+        load_tables(2, 0)
+        load_scales(*scale_runs[2])
+        load_tables(3, 0)
+        load_words(K, 0)
+        load_words(K, ROT)
+        load_scales(*scale_runs[3])
+        load_scales(*scale_runs[4])
+        load_words(Q, N)
+        load_words(Q, ROT + N)
+        for t in range(TILES):
+            load_tables(t, 1)
+        load_words(K, N)
+        load_words(K, ROT + N)
+
+        def quantize_tokens(t):
+            sources = {}
+            for kh in range(2):
+                pairs = x_raw[t, kh][:].bitcast(F32)
+                if t == 0:
+                    sources[kh] = pairs.rearrange("p (g i u) -> p g u i", g=2, u=2)
+                else:
+                    ordered = stage.tile([P, 2, 2, P], F32, name="ordered", align_bytes=64)
+                    nc.scalar.copy(out=ordered[:], in_=pairs.rearrange("p (g i u) -> p g u i", g=2, u=2))
+                    sources[kh] = ordered
+            banks = {}
+            for kh in range(2):
+                bank = tr_psum.tile([P, 2, 2, P], F32, name="tr_bank")
+                for g in range(2):
+                    for u in range(2):
+                        nc.tensor.transpose(bank[:, g, u, :], sources[kh][:, g, u, :], ident[:])
+                banks[kh] = bank
+            for kh in range(2):
+                grouped = stage.tile([P, K_HALF], BF16, name="grouped", align_bytes=64)
+                nc.scalar.copy(
+                    out=grouped[:].bitcast(F32).rearrange("p (g r u) -> p g r u", g=2, u=2),
+                    in_=banks[kh][:].rearrange("p g u r -> p g r u"),
+                )
+                codes = keep.tile([P, 2 * P], U32, name=f"x_codes_{t}_{kh}", align_bytes=64)
+                scales = keep.tile([P, 2 * P], U8, name=f"x_scales_{t}_{kh}", align_bytes=64)
+                nc.vector.quantize_mx(out=codes[:].bitcast(E5M2X4), scales=scales[:], in_=grouped[:])
+                x_codes[t, kh], x_scales[t, kh] = codes, scales
+
+        def project(t, m, col):
+            acc = mx_psum.tile([P, N], F32, name="acc")
+            for g in range(PASSES):
+                tokens = slice((g % 2) * P, (g % 2 + 1) * P)
+                nc.tensor.matmul_mx(
+                    out=acc[:],
+                    lhsT=x_codes[t, g // 2][:, tokens].bitcast(E5M2X4),
+                    lhsT_scale=x_scales[t, g // 2][:, tokens],
+                    rhs=w_words[m, col][:, g, :].bitcast(E2M1X4),
+                    rhs_scale=w_scales[m, col][:, g, :],
+                    start=(g == 0),
+                    stop=(g == PASSES - 1),
+                )
+            return acc
+
+        steps = [(c, m, t) for c in range(2) for m in (Q, K) for t in range(TILES)]
+        quantize_tokens(0)
+        for i, (c, m, t) in enumerate(steps):
+            with_cos = keep.tile([P, 2, N], F32, name=f"with_cos_{i}", align_bytes=64)
+            with_sin = stage.tile([P, 2, N], F32, name="with_sin", align_bytes=64)
+            cos_t, sin_t = cos_sb[t, c], sin_sb[t, c]
+
+            low = project(t, m, c * N)
+            nc.vector.tensor_tensor(out=with_cos[:, 0, :], in0=low[:], in1=cos_t[:, 0, :], op=MULT)
+            nc.vector.tensor_tensor(out=with_sin[:, 1, :], in0=low[:], in1=sin_t[:, 1, :], op=MULT)
+            if i + 1 < TILES:
+                quantize_tokens(i + 1)
+            high = project(t, m, ROT + c * N)
+            nc.vector.tensor_tensor(out=with_cos[:, 1, :], in0=high[:], in1=cos_t[:, 1, :], op=MULT)
+            nc.vector.scalar_tensor_tensor(
+                out=with_sin[:, 0, :], in0=high[:], scalar=-1.0, in1=sin_t[:, 0, :], op0=MULT, op1=MULT
+            )
+
+            dest = paired(outs[m][0, t * P:(t + 1) * P, :], c)
+            if i + 1 < len(steps):
+                nc.gpsimd.tensor_tensor(out=with_cos[:], in0=with_cos[:], in1=with_sin[:], op=ADD)
+                nc.sync.dma_start(out=dest, in_=with_cos[:])
+            else:
+                for half in (1, 0):
+                    nc.vector.tensor_tensor(
+                        out=with_cos[:, half, :], in0=with_cos[:, half, :], in1=with_sin[:, half, :], op=ADD
+                    )
+                    nc.sync.dma_start(out=dest[:, half, :], in_=with_cos[:, half, :])

@@ -34,6 +34,7 @@ def tile_attention_pa_kernel(tc, x, cos, sin, Wq_words, Wq_scales, Wk_words, Wk_
     with ExitStack() as ctx:
         keep = ctx.enter_context(tc.tile_pool(name="keep", bufs=1))
         stage = ctx.enter_context(tc.tile_pool(name="stage", bufs=3))
+        products = ctx.enter_context(tc.tile_pool(name="products", bufs=4))
         tr_psum = ctx.enter_context(tc.psum_pool(name="tr_psum", bufs=2))
         mx_psum = ctx.enter_context(tc.psum_pool(name="mx_psum", bufs=6))
         ctx.enter_context(tc.manual_schedule())
@@ -52,9 +53,9 @@ def tile_attention_pa_kernel(tc, x, cos, sin, Wq_words, Wq_scales, Wk_words, Wk_
             for c0 in range(col, col + width, N):
                 w_scales[m, c0] = plane[:, :, c0 - col:c0 - col + N]
 
-        def load_scales(m, col, width):
+        def load_scales(queue, m, col, width):
             for r in range(4):
-                nc.sync.dma_start(
+                queue.dma_start(
                     out=planes[m, col][r:P:32, :, :].bitcast(I32),
                     in_=w_scales_hbm[m][:, r:16:4, col:col + width].rearrange("g q n -> q g n").bitcast(I32),
                 )
@@ -67,11 +68,19 @@ def tile_attention_pa_kernel(tc, x, cos, sin, Wq_words, Wq_scales, Wk_words, Wk_
             )
             w_words[m, col] = words
 
-        def load_x(t):
-            for kh in range(2):
-                raw = keep.tile([P, K_HALF], BF16, name=f"x_{t}_{kh}", align_bytes=64)
-                nc.sync.dma_start(out=raw[:], in_=x[0, t * P:(t + 1) * P, kh * K_HALF:(kh + 1) * K_HALF])
-                x_raw[t, kh] = raw
+        def load_all_words(m):
+            words = keep.tile([P, PASSES, 2 * D], U8, name=f"words_{m}", align_bytes=64)
+            for g in range(PASSES):
+                nc.sync.dma_start(out=words[:, g, :].bitcast(I32), in_=w_words_hbm[m][g].bitcast(I32))
+            for col in range(0, D, N):
+                w_words[m, col] = words[:, :, 2 * col:2 * (col + N)]
+
+        def load_x(t, pieces):
+            raw = keep.tile([P, D], BF16, name=f"x_{t}", align_bytes=64)
+            for k0 in range(0, D, D // pieces):
+                k_cols = slice(k0, k0 + D // pieces)
+                nc.sync.dma_start(out=raw[:, k_cols], in_=x[0, t * P:(t + 1) * P, k_cols])
+            x_raw[t] = raw
 
         def load_tables(t, c):
             for name, table, tiles in (("cos", cos, cos_sb), ("sin", sin, sin_sb)):
@@ -82,38 +91,31 @@ def tile_attention_pa_kernel(tc, x, cos, sin, Wq_words, Wq_scales, Wk_words, Wk_
         ident = keep.tile([P, P], F32, name="ident", align_bytes=64)
         make_identity(nc, ident[:])
 
-        scale_runs = [(Q, 0, N), (Q, ROT, N), (K, 0, D), (Q, N, N), (Q, ROT + N, N)]
-        for run in scale_runs:
-            zero_plane(*run)
+        first_run, q_run, k_run = (Q, 0, N), (Q, N, D - N), (K, 0, D)
+        zero_plane(*first_run)
+        zero_plane(*q_run)
+        load_scales(nc.gpsimd, *q_run)
 
-        load_x(0)
-        load_scales(*scale_runs[0])
+        load_x(0, 2)
+        load_scales(nc.sync, *first_run)
         load_words(Q, 0)
-        load_x(1)
+        load_x(1, 1)
         load_tables(0, 0)
-        load_scales(*scale_runs[1])
         load_words(Q, ROT)
-        load_x(2)
-        load_tables(1, 0)
-        load_x(3)
-        load_tables(2, 0)
-        load_scales(*scale_runs[2])
-        load_tables(3, 0)
-        load_words(K, 0)
-        load_words(K, ROT)
-        load_scales(*scale_runs[3])
-        load_scales(*scale_runs[4])
+        for t in range(1, TILES):
+            if t + 1 < TILES:
+                load_x(t + 1, 1)
+            load_tables(t, 0)
         load_words(Q, N)
         load_words(Q, ROT + N)
         for t in range(TILES):
             load_tables(t, 1)
-        load_words(K, N)
-        load_words(K, ROT + N)
+        load_all_words(K)
 
         def quantize_tokens(t):
             sources = {}
             for kh in range(2):
-                pairs = x_raw[t, kh][:].bitcast(F32)
+                pairs = x_raw[t][:, kh * K_HALF:(kh + 1) * K_HALF].bitcast(F32)
                 if t == 0:
                     sources[kh] = pairs.rearrange("p (g i u) -> p g u i", g=2, u=2)
                 else:
@@ -153,11 +155,15 @@ def tile_attention_pa_kernel(tc, x, cos, sin, Wq_words, Wq_scales, Wk_words, Wk_
                 )
             return acc
 
-        steps = [(c, m, t) for c in range(2) for m in (Q, K) for t in range(TILES)]
+        steps = [(Q, t, c) for c in range(2) for t in range(TILES)]
+        steps += [(K, t, c) for t in range(TILES) for c in range(2)]
+        results = {}
         quantize_tokens(0)
-        for i, (c, m, t) in enumerate(steps):
-            with_cos = keep.tile([P, 2, N], F32, name=f"with_cos_{i}", align_bytes=64)
-            with_sin = stage.tile([P, 2, N], F32, name="with_sin", align_bytes=64)
+        zero_plane(*k_run)
+        load_scales(nc.gpsimd, *k_run)
+        for i, (m, t, c) in enumerate(steps):
+            with_cos = products.tile([P, 2, N], F32, name="with_cos", align_bytes=64)
+            with_sin = products.tile([P, 2, N], F32, name="with_sin", align_bytes=64)
             cos_t, sin_t = cos_sb[t, c], sin_sb[t, c]
 
             low = project(t, m, c * N)
@@ -171,13 +177,19 @@ def tile_attention_pa_kernel(tc, x, cos, sin, Wq_words, Wq_scales, Wk_words, Wk_
                 out=with_sin[:, 0, :], in0=high[:], scalar=-1.0, in1=sin_t[:, 0, :], op0=MULT, op1=MULT
             )
 
-            dest = paired(outs[m][0, t * P:(t + 1) * P, :], c)
+            if c == 0:
+                results[m, t] = keep.tile([P, D], F32, name=f"result_{m}_{t}", align_bytes=64)
+            result = results[m, t]
+            rows = outs[m][0, t * P:(t + 1) * P, :]
             if i + 1 < len(steps):
-                nc.gpsimd.tensor_tensor(out=with_cos[:], in0=with_cos[:], in1=with_sin[:], op=ADD)
-                nc.sync.dma_start(out=dest, in_=with_cos[:])
+                nc.gpsimd.tensor_tensor(out=paired(result[:], c), in0=with_cos[:], in1=with_sin[:], op=ADD)
+                if i + 2 == len(steps):
+                    nc.sync.dma_start(out=paired(rows, c), in_=paired(result[:], c))
+                elif c == 1:
+                    nc.sync.dma_start(out=rows, in_=result[:])
             else:
                 for half in (1, 0):
                     nc.vector.tensor_tensor(
                         out=with_cos[:, half, :], in0=with_cos[:, half, :], in1=with_sin[:, half, :], op=ADD
                     )
-                    nc.sync.dma_start(out=dest[:, half, :], in_=with_cos[:, half, :])
+                    nc.sync.dma_start(out=paired(rows, c)[:, half, :], in_=with_cos[:, half, :])

@@ -14,7 +14,7 @@ U8 = mybir.dt.uint8
 E5M2X4 = mybir.dt.float8_e5m2_x4
 E2M1X4 = mybir.dt.float4_e2m1fn_x4
 MULT = mybir.AluOpType.mult
-ADD = mybir.AluOpType.add
+SUB = mybir.AluOpType.subtract
 
 P = 128
 PASSES = 4
@@ -22,7 +22,12 @@ K_HALF = D // 2
 N = 512
 ROT = D // 2
 TILES = S // P
+WHOLE_ROW_TILES = 3
 Q, K = 0, 1
+LOW, HIGH = 0, 1
+LAST_STEPS = 3
+COS_LOW, COS_HIGH, SIN_LOW, SIN_HIGH = 0, 1, 2, 3
+PARTS = {HIGH: slice(COS_HIGH, SIN_LOW + 1), LOW: slice(COS_LOW, SIN_HIGH + 1, SIN_HIGH - COS_LOW)}
 
 
 def tile_attention_pa_kernel(tc, x, cos, sin, Wq_words, Wq_scales, Wk_words, Wk_scales, out_0, out_1):
@@ -33,47 +38,40 @@ def tile_attention_pa_kernel(tc, x, cos, sin, Wq_words, Wq_scales, Wk_words, Wk_
 
     with ExitStack() as ctx:
         keep = ctx.enter_context(tc.tile_pool(name="keep", bufs=1))
-        stage = ctx.enter_context(tc.tile_pool(name="stage", bufs=3))
-        products = ctx.enter_context(tc.tile_pool(name="products", bufs=4))
-        tr_psum = ctx.enter_context(tc.psum_pool(name="tr_psum", bufs=2))
-        mx_psum = ctx.enter_context(tc.psum_pool(name="mx_psum", bufs=6))
+        stage = ctx.enter_context(tc.tile_pool(name="stage", bufs=2))
+        products = ctx.enter_context(tc.tile_pool(name="products", bufs=5))
+        psum = ctx.enter_context(tc.psum_pool(name="psum", bufs=8))
         ctx.enter_context(tc.manual_schedule())
 
-        x_raw, x_codes, x_scales = {}, {}, {}
-        w_words, w_scales, planes = {}, {}, {}
-        cos_sb, sin_sb = {}, {}
+        x_raw, x_words, x_grouped, x_codes, x_scales = {}, {}, {}, {}, {}
+        w_words, w_scales = {}, {}
+        table_pairs, tables = {}, {}
+        accs, prods, results = {}, {}, {}
 
         def paired(rows, c):
             return rows.rearrange("p (half n) -> p half n", half=2)[:, :, c * N:(c + 1) * N]
 
-        def zero_plane(m, col, width):
-            plane = keep.tile([P, PASSES, width], U8, name=f"plane_{m}_{col}", align_bytes=64)
+        def zero_plane(m, col):
+            plane = keep.tile([P, PASSES, N], U8, name=f"plane_{m}_{col}", align_bytes=64)
             nc.vector.memset(plane[:].rearrange("p g n -> p (g n)").bitcast(I32), 0)
-            planes[m, col] = plane
-            for c0 in range(col, col + width, N):
-                w_scales[m, c0] = plane[:, :, c0 - col:c0 - col + N]
+            w_scales[m, col] = plane
 
-        def load_scales(queue, m, col, width):
+        def load_scales(m, col):
             for r in range(4):
-                queue.dma_start(
-                    out=planes[m, col][r:P:32, :, :].bitcast(I32),
-                    in_=w_scales_hbm[m][:, r:16:4, col:col + width].rearrange("g q n -> q g n").bitcast(I32),
+                nc.sync.dma_start(
+                    out=w_scales[m, col][r:P:32, :, :].bitcast(I32),
+                    in_=w_scales_hbm[m][:, r:16:4, col:col + N].rearrange("g q n -> q g n").bitcast(I32),
                 )
 
-        def load_words(m, col):
+        def load_words(m, c, half):
+            col = half * ROT + c * N
+            load_scales(m, col)
             words = keep.tile([P, PASSES, 2 * N], U8, name=f"words_{m}_{col}", align_bytes=64)
             nc.sync.dma_start(
                 out=words[:].bitcast(I32),
                 in_=w_words_hbm[m][:, :, 2 * col:2 * (col + N)].rearrange("g p n -> p g n").bitcast(I32),
             )
             w_words[m, col] = words
-
-        def load_all_words(m):
-            words = keep.tile([P, PASSES, 2 * D], U8, name=f"words_{m}", align_bytes=64)
-            for g in range(PASSES):
-                nc.sync.dma_start(out=words[:, g, :].bitcast(I32), in_=w_words_hbm[m][g].bitcast(I32))
-            for col in range(0, D, N):
-                w_words[m, col] = words[:, :, 2 * col:2 * (col + N)]
 
         def load_x(t, pieces):
             raw = keep.tile([P, D], BF16, name=f"x_{t}", align_bytes=64)
@@ -82,114 +80,170 @@ def tile_attention_pa_kernel(tc, x, cos, sin, Wq_words, Wq_scales, Wk_words, Wk_
                 nc.sync.dma_start(out=raw[:, k_cols], in_=x[0, t * P:(t + 1) * P, k_cols])
             x_raw[t] = raw
 
-        def load_tables(t, c):
-            for name, table, tiles in (("cos", cos, cos_sb), ("sin", sin, sin_sb)):
-                tile = keep.tile([P, 2, N], BF16, name=f"{name}_{t}_{c}", align_bytes=64)
-                nc.sync.dma_start(out=tile[:], in_=paired(table[t * P:(t + 1) * P, :], c))
-                tiles[t, c] = tile
+        def load_table_part(t0, c, part):
+            if (t0, c) not in tables:
+                tile = keep.tile([P, 2, 4, N], BF16, name=f"tables_{t0}_{c}", align_bytes=64)
+                for j in range(2):
+                    tables[t0 + j, c] = tile[:, j, :, :]
+                table_pairs[t0, c] = tile
+            table = cos if part in (COS_LOW, COS_HIGH) else sin
+            col = (ROT if part in (COS_HIGH, SIN_HIGH) else 0) + c * N
+            rows = table[t0 * P:(t0 + 2) * P, col:col + N]
+            nc.sync.dma_start(out=table_pairs[t0, c][:, :, part, :], in_=rows.rearrange("(j p) n -> p j n", p=P))
 
-        ident = keep.tile([P, P], F32, name="ident", align_bytes=64)
-        make_identity(nc, ident[:])
+        def negate_sin_high(t0, c):
+            part = table_pairs[t0, c][:, :, SIN_HIGH, :]
+            if (t0, c) == (0, 0):
+                nc.vector.tensor_scalar_mul(part, part, -1.0)
+            else:
+                nc.scalar.mul(out=part, in_=part, mul=-1.0)
 
-        first_run, q_run, k_run = (Q, 0, N), (Q, N, D - N), (K, 0, D)
-        zero_plane(*first_run)
-        zero_plane(*q_run)
-        load_scales(nc.gpsimd, *q_run)
-
-        load_x(0, 2)
-        load_scales(nc.sync, *first_run)
-        load_words(Q, 0)
-        load_x(1, 1)
-        load_tables(0, 0)
-        load_words(Q, ROT)
-        for t in range(1, TILES):
-            if t + 1 < TILES:
-                load_x(t + 1, 1)
-            load_tables(t, 0)
-        load_words(Q, N)
-        load_words(Q, ROT + N)
-        for t in range(TILES):
-            load_tables(t, 1)
-        load_all_words(K)
-
-        def quantize_tokens(t):
-            sources = {}
+        def order_words(t, copy):
             for kh in range(2):
                 pairs = x_raw[t][:, kh * K_HALF:(kh + 1) * K_HALF].bitcast(F32)
-                if t == 0:
-                    sources[kh] = pairs.rearrange("p (g i u) -> p g u i", g=2, u=2)
+                pairs = pairs.rearrange("p (g i u) -> p g u i", g=2, u=2)
+                if copy is None:
+                    x_words[t, kh] = pairs
                 else:
-                    ordered = stage.tile([P, 2, 2, P], F32, name="ordered", align_bytes=64)
-                    nc.scalar.copy(out=ordered[:], in_=pairs.rearrange("p (g i u) -> p g u i", g=2, u=2))
-                    sources[kh] = ordered
+                    ordered = stage.tile([P, 2, 2, P], F32, name="ordered", align_bytes=64, bufs=4)
+                    copy(out=ordered[:], in_=pairs)
+                    x_words[t, kh] = ordered
+
+        def transpose_tokens(t):
+            grouped = stage.tile([P, D], BF16, name="grouped", align_bytes=64)
             banks = {}
             for kh in range(2):
-                bank = tr_psum.tile([P, 2, 2, P], F32, name="tr_bank")
+                bank = psum.tile([P, 2, 2, P], F32, name="bank")
                 for g in range(2):
                     for u in range(2):
-                        nc.tensor.transpose(bank[:, g, u, :], sources[kh][:, g, u, :], ident[:])
+                        nc.tensor.transpose(bank[:, g, u, :], x_words[t, kh][:, g, u, :], ident[:])
                 banks[kh] = bank
             for kh in range(2):
-                grouped = stage.tile([P, K_HALF], BF16, name="grouped", align_bytes=64)
                 nc.scalar.copy(
-                    out=grouped[:].bitcast(F32).rearrange("p (g r u) -> p g r u", g=2, u=2),
+                    out=grouped[:, kh * K_HALF:(kh + 1) * K_HALF].bitcast(F32).rearrange("p (g r u) -> p g r u", g=2, u=2),
                     in_=banks[kh][:].rearrange("p g u r -> p g r u"),
                 )
-                codes = keep.tile([P, 2 * P], U32, name=f"x_codes_{t}_{kh}", align_bytes=64)
-                scales = keep.tile([P, 2 * P], U8, name=f"x_scales_{t}_{kh}", align_bytes=64)
-                nc.vector.quantize_mx(out=codes[:].bitcast(E5M2X4), scales=scales[:], in_=grouped[:])
-                x_codes[t, kh], x_scales[t, kh] = codes, scales
+            x_grouped[t] = grouped
 
-        def project(t, m, col):
-            acc = mx_psum.tile([P, N], F32, name="acc")
+        def quantize_tokens(t, pieces):
+            codes = keep.tile([P, PASSES * P], U32, name=f"x_codes_{t}", align_bytes=64)
+            scales = keep.tile([P, PASSES * P], U8, name=f"x_scales_{t}", align_bytes=64)
+            width = PASSES * P // pieces
+            for w0 in range(0, PASSES * P, width):
+                nc.vector.quantize_mx(
+                    out=codes[:, w0:w0 + width].bitcast(E5M2X4),
+                    scales=scales[:, w0:w0 + width],
+                    in_=x_grouped[t][:, 4 * w0:4 * (w0 + width)],
+                )
+            x_codes[t], x_scales[t] = codes, scales
+
+        def project(m, c, t, half):
+            col = half * ROT + c * N
+            acc = psum.tile([P, N], F32, name="bank")
             for g in range(PASSES):
-                tokens = slice((g % 2) * P, (g % 2 + 1) * P)
+                tokens = slice(g * P, (g + 1) * P)
                 nc.tensor.matmul_mx(
                     out=acc[:],
-                    lhsT=x_codes[t, g // 2][:, tokens].bitcast(E5M2X4),
-                    lhsT_scale=x_scales[t, g // 2][:, tokens],
+                    lhsT=x_codes[t][:, tokens].bitcast(E5M2X4),
+                    lhsT_scale=x_scales[t][:, tokens],
                     rhs=w_words[m, col][:, g, :].bitcast(E2M1X4),
                     rhs_scale=w_scales[m, col][:, g, :],
                     start=(g == 0),
                     stop=(g == PASSES - 1),
                 )
-            return acc
+            accs[m, c, t, half] = acc
 
-        steps = [(Q, t, c) for c in range(2) for t in range(TILES)]
-        steps += [(K, t, c) for t in range(TILES) for c in range(2)]
-        results = {}
-        quantize_tokens(0)
-        zero_plane(*k_run)
-        load_scales(nc.gpsimd, *k_run)
-        for i, (m, t, c) in enumerate(steps):
-            with_cos = products.tile([P, 2, N], F32, name="with_cos", align_bytes=64)
-            with_sin = products.tile([P, 2, N], F32, name="with_sin", align_bytes=64)
-            cos_t, sin_t = cos_sb[t, c], sin_sb[t, c]
-
-            low = project(t, m, c * N)
-            nc.vector.tensor_tensor(out=with_cos[:, 0, :], in0=low[:], in1=cos_t[:, 0, :], op=MULT)
-            nc.vector.tensor_tensor(out=with_sin[:, 1, :], in0=low[:], in1=sin_t[:, 1, :], op=MULT)
-            if i + 1 < TILES:
-                quantize_tokens(i + 1)
-            high = project(t, m, ROT + c * N)
-            nc.vector.tensor_tensor(out=with_cos[:, 1, :], in0=high[:], in1=cos_t[:, 1, :], op=MULT)
-            nc.vector.scalar_tensor_tensor(
-                out=with_sin[:, 0, :], in0=high[:], scalar=-1.0, in1=sin_t[:, 0, :], op0=MULT, op1=MULT
+        def multiply(m, c, t, half):
+            if half == HIGH:
+                prods[m, c, t] = products.tile([P, 4, N], F32, name="prod", align_bytes=64)
+            nc.vector.tensor_tensor(
+                out=prods[m, c, t][:, PARTS[half], :],
+                in0=accs[m, c, t, half][:].unsqueeze(1).to_broadcast([P, 2, N]),
+                in1=tables[t, c][:, PARTS[half], :],
+                op=MULT,
             )
 
-            if c == 0:
-                results[m, t] = keep.tile([P, D], F32, name=f"result_{m}_{t}", align_bytes=64)
-            result = results[m, t]
-            rows = outs[m][0, t * P:(t + 1) * P, :]
-            if i + 1 < len(steps):
-                nc.gpsimd.tensor_tensor(out=paired(result[:], c), in0=with_cos[:], in1=with_sin[:], op=ADD)
-                if i + 2 == len(steps):
-                    nc.sync.dma_start(out=paired(rows, c), in_=paired(result[:], c))
-                elif c == 1:
-                    nc.sync.dma_start(out=rows, in_=result[:])
+        def subtract(m, c, t):
+            if m == Q and t < WHOLE_ROW_TILES:
+                if c == 0:
+                    results[Q, t] = keep.tile([P, D], F32, name=f"q_rows_{t}", align_bytes=64)
+                dest = paired(results[Q, t][:], c)
             else:
-                for half in (1, 0):
-                    nc.vector.tensor_tensor(
-                        out=with_cos[:, half, :], in0=with_cos[:, half, :], in1=with_sin[:, half, :], op=ADD
-                    )
-                    nc.sync.dma_start(out=paired(rows, c)[:, half, :], in_=with_cos[:, half, :])
+                results[m, c, t] = keep.tile([P, 2, N], F32, name=f"block_{m}_{c}_{t}", align_bytes=64)
+                dest = results[m, c, t][:]
+            prod = prods[m, c, t]
+            nc.gpsimd.tensor_tensor(out=dest, in0=prod[:, 0:2, :], in1=prod[:, 2:4, :], op=SUB)
+
+        def store(m, c, t):
+            rows = outs[m][0, t * P:(t + 1) * P, :]
+            if m == Q and t < WHOLE_ROW_TILES:
+                if c == 1:
+                    nc.sync.dma_start(out=rows, in_=results[Q, t][:])
+            else:
+                nc.sync.dma_start(out=paired(rows, c), in_=results[m, c, t][:])
+
+        def subtract_half_and_store(engine, m, c, t, half):
+            rows = paired(outs[m][0, t * P:(t + 1) * P, :], c)
+            prod = prods[m, c, t]
+            engine.tensor_tensor(out=prod[:, half, :], in0=prod[:, half, :], in1=prod[:, 2 + half, :], op=SUB)
+            nc.sync.dma_start(out=rows[:, half, :], in_=prod[:, half, :])
+
+        ident = keep.tile([P, P], F32, name="ident", align_bytes=64)
+        make_identity(nc, ident[:])
+        for c in range(2):
+            for m in (Q, K):
+                for half in (HIGH, LOW):
+                    zero_plane(m, half * ROT + c * N)
+
+        load_x(0, 2)
+        load_x(1, 1)
+        load_x(2, 1)
+        for c in range(2):
+            load_words(Q, c, HIGH)
+            if c == 0:
+                load_x(3, 1)
+            load_table_part(0, c, COS_HIGH)
+            load_table_part(0, c, SIN_LOW)
+            load_words(Q, c, LOW)
+            load_table_part(0, c, SIN_HIGH)
+            load_table_part(0, c, COS_LOW)
+            for part in (SIN_HIGH, COS_HIGH, SIN_LOW, COS_LOW):
+                load_table_part(2, c, part)
+            load_words(K, c, HIGH)
+            load_words(K, c, LOW)
+
+        order_words(0, None)
+        order_words(1, nc.vector.tensor_copy)
+        order_words(2, nc.vector.tensor_copy)
+        for t in range(2):
+            transpose_tokens(t)
+            quantize_tokens(t, 2)
+        transpose_tokens(2)
+        order_words(3, nc.vector.tensor_copy)
+        quantize_tokens(2, 2)
+
+        steps = [(m, c, t) for c in range(2) for m in (Q, K) for t in range(TILES)]
+        by_halves = steps[-LAST_STEPS:]
+        banks = []
+        for c in range(2):
+            for m in (Q, K):
+                if c == 0:
+                    banks += [(m, c, t, half) for half in (HIGH, LOW) for t in range(2)]
+                    banks += [(m, c, t, half) for t in range(2, TILES) for half in (HIGH, LOW)]
+                else:
+                    banks += [(m, c, t, half) for t in range(TILES) for half in (HIGH, LOW)]
+        for m, c, t, half in banks:
+            if (m, c, t, half) == (Q, 0, 1, HIGH):
+                transpose_tokens(3)
+                quantize_tokens(3, 2)
+            if m == Q and half == LOW and t % 2 == 0:
+                negate_sin_high(t, c)
+            project(m, c, t, half)
+            multiply(m, c, t, half)
+            if half == LOW and (m, c, t) not in by_halves:
+                subtract(m, c, t)
+                store(m, c, t)
+        last_halves = [(*step, half) for step in by_halves for half in (LOW, HIGH)]
+        subtract_half_and_store(nc.gpsimd, *last_halves[0])
+        for piece in last_halves[1:]:
+            subtract_half_and_store(nc.vector, *piece)

@@ -17,17 +17,21 @@ MULT = mybir.AluOpType.mult
 SUB = mybir.AluOpType.subtract
 
 P = 128
-PASSES = 4
+PACK = 4
+PASSES = D // (P * PACK)
 K_HALF = D // 2
 N = 512
 ROT = D // 2
+BLOCKS = ROT // N
 TILES = S // P
-WHOLE_ROW_TILES = 3
 Q, K = 0, 1
 LOW, HIGH = 0, 1
-LAST_STEPS = 3
+
 COS_LOW, COS_HIGH, SIN_LOW, SIN_HIGH = 0, 1, 2, 3
 PARTS = {HIGH: slice(COS_HIGH, SIN_LOW + 1), LOW: slice(COS_LOW, SIN_HIGH + 1, SIN_HIGH - COS_LOW)}
+
+LAST_STEPS = 3
+PRODUCT_BUFS = 5
 
 
 def tile_attention_pa_kernel(tc, x, cos, sin, Wq_words, Wq_scales, Wk_words, Wk_scales, out_0, out_1):
@@ -39,39 +43,35 @@ def tile_attention_pa_kernel(tc, x, cos, sin, Wq_words, Wq_scales, Wk_words, Wk_
     with ExitStack() as ctx:
         keep = ctx.enter_context(tc.tile_pool(name="keep", bufs=1))
         stage = ctx.enter_context(tc.tile_pool(name="stage", bufs=2))
-        products = ctx.enter_context(tc.tile_pool(name="products", bufs=5))
+        products = ctx.enter_context(tc.tile_pool(name="products", bufs=PRODUCT_BUFS))
         psum = ctx.enter_context(tc.psum_pool(name="psum", bufs=8))
         ctx.enter_context(tc.manual_schedule())
 
         x_raw, x_words, x_grouped, x_codes, x_scales = {}, {}, {}, {}, {}
-        w_words, w_scales = {}, {}
-        table_pairs, tables = {}, {}
+        w_words, w_scales, tables = {}, {}, {}
         accs, prods, results = {}, {}, {}
 
         def paired(rows, c):
             return rows.rearrange("p (half n) -> p half n", half=2)[:, :, c * N:(c + 1) * N]
 
-        def zero_plane(m, col):
-            plane = keep.tile([P, PASSES, N], U8, name=f"plane_{m}_{col}", align_bytes=64)
-            nc.vector.memset(plane[:].rearrange("p g n -> p (g n)").bitcast(I32), 0)
-            w_scales[m, col] = plane
+        def zero_scales(m, c, half):
+            scales = keep.tile([P, PASSES, N], U8, name=f"w_scales_{m}_{c}_{half}", align_bytes=64)
+            nc.vector.memset(scales[:].rearrange("p g n -> p (g n)").bitcast(I32), 0)
+            w_scales[m, c, half] = scales
 
-        def load_scales(m, col):
+        def load_weights(m, c, half):
+            col = half * ROT + c * N
             for r in range(4):
                 nc.sync.dma_start(
-                    out=w_scales[m, col][r:P:32, :, :].bitcast(I32),
+                    out=w_scales[m, c, half][r:P:32, :, :].bitcast(I32),
                     in_=w_scales_hbm[m][:, r:16:4, col:col + N].rearrange("g q n -> q g n").bitcast(I32),
                 )
-
-        def load_words(m, c, half):
-            col = half * ROT + c * N
-            load_scales(m, col)
-            words = keep.tile([P, PASSES, 2 * N], U8, name=f"words_{m}_{col}", align_bytes=64)
+            words = keep.tile([P, PASSES, 2 * N], U8, name=f"w_words_{m}_{c}_{half}", align_bytes=64)
             nc.sync.dma_start(
                 out=words[:].bitcast(I32),
                 in_=w_words_hbm[m][:, :, 2 * col:2 * (col + N)].rearrange("g p n -> p g n").bitcast(I32),
             )
-            w_words[m, col] = words
+            w_words[m, c, half] = words
 
         def load_x(t, pieces):
             raw = keep.tile([P, D], BF16, name=f"x_{t}", align_bytes=64)
@@ -80,33 +80,33 @@ def tile_attention_pa_kernel(tc, x, cos, sin, Wq_words, Wq_scales, Wk_words, Wk_
                 nc.sync.dma_start(out=raw[:, k_cols], in_=x[0, t * P:(t + 1) * P, k_cols])
             x_raw[t] = raw
 
-        def load_table_part(t0, c, part):
-            if (t0, c) not in tables:
-                tile = keep.tile([P, 2, 4, N], BF16, name=f"tables_{t0}_{c}", align_bytes=64)
-                for j in range(2):
-                    tables[t0 + j, c] = tile[:, j, :, :]
-                table_pairs[t0, c] = tile
-            table = cos if part in (COS_LOW, COS_HIGH) else sin
-            col = (ROT if part in (COS_HIGH, SIN_HIGH) else 0) + c * N
-            rows = table[t0 * P:(t0 + 2) * P, col:col + N]
-            nc.sync.dma_start(out=table_pairs[t0, c][:, :, part, :], in_=rows.rearrange("(j p) n -> p j n", p=P))
+        def load_table_parts(t, c, first, last):
+            if (t, c) not in tables:
+                tables[t, c] = keep.tile([P, 4, N], BF16, name=f"tables_{t}_{c}", align_bytes=64)
+            table = cos if first in (COS_LOW, COS_HIGH) else sin
+            halves = paired(table[t * P:(t + 1) * P, :], c)
+            nc.sync.dma_start(out=tables[t, c][:, first:last + 1, :], in_=halves[:, first % 2:last % 2 + 1, :])
 
-        def negate_sin_high(t0, c):
-            part = table_pairs[t0, c][:, :, SIN_HIGH, :]
-            if (t0, c) == (0, 0):
+        def load_tables(t, c):
+            load_table_parts(t, c, SIN_LOW, SIN_HIGH)
+            load_table_parts(t, c, COS_LOW, COS_HIGH)
+
+        def negate_sin_high(t, c):
+            part = tables[t, c][:, SIN_HIGH, :]
+            if (t, c) == (0, 0):
                 nc.vector.tensor_scalar_mul(part, part, -1.0)
             else:
                 nc.scalar.mul(out=part, in_=part, mul=-1.0)
 
-        def order_words(t, copy):
+        def order_words(t):
             for kh in range(2):
-                pairs = x_raw[t][:, kh * K_HALF:(kh + 1) * K_HALF].bitcast(F32)
-                pairs = pairs.rearrange("p (g i u) -> p g u i", g=2, u=2)
-                if copy is None:
-                    x_words[t, kh] = pairs
+                words = x_raw[t][:, kh * K_HALF:(kh + 1) * K_HALF].bitcast(F32)
+                words = words.rearrange("p (g i u) -> p g u i", g=2, u=2)
+                if t == 0:
+                    x_words[t, kh] = words
                 else:
                     ordered = stage.tile([P, 2, 2, P], F32, name="ordered", align_bytes=64, bufs=4)
-                    copy(out=ordered[:], in_=pairs)
+                    nc.vector.tensor_copy(out=ordered[:], in_=words)
                     x_words[t, kh] = ordered
 
         def transpose_tokens(t):
@@ -119,26 +119,26 @@ def tile_attention_pa_kernel(tc, x, cos, sin, Wq_words, Wq_scales, Wk_words, Wk_
                         nc.tensor.transpose(bank[:, g, u, :], x_words[t, kh][:, g, u, :], ident[:])
                 banks[kh] = bank
             for kh in range(2):
+                half_of_k = grouped[:, kh * K_HALF:(kh + 1) * K_HALF].bitcast(F32)
                 nc.scalar.copy(
-                    out=grouped[:, kh * K_HALF:(kh + 1) * K_HALF].bitcast(F32).rearrange("p (g r u) -> p g r u", g=2, u=2),
+                    out=half_of_k.rearrange("p (g r u) -> p g r u", g=2, u=2),
                     in_=banks[kh][:].rearrange("p g u r -> p g r u"),
                 )
             x_grouped[t] = grouped
 
-        def quantize_tokens(t, pieces):
+        def quantize_tokens(t):
             codes = keep.tile([P, PASSES * P], U32, name=f"x_codes_{t}", align_bytes=64)
             scales = keep.tile([P, PASSES * P], U8, name=f"x_scales_{t}", align_bytes=64)
-            width = PASSES * P // pieces
-            for w0 in range(0, PASSES * P, width):
+            for kh in range(2):
+                cols = slice(kh * K_HALF // PACK, (kh + 1) * K_HALF // PACK)
                 nc.vector.quantize_mx(
-                    out=codes[:, w0:w0 + width].bitcast(E5M2X4),
-                    scales=scales[:, w0:w0 + width],
-                    in_=x_grouped[t][:, 4 * w0:4 * (w0 + width)],
+                    out=codes[:, cols].bitcast(E5M2X4),
+                    scales=scales[:, cols],
+                    in_=x_grouped[t][:, kh * K_HALF:(kh + 1) * K_HALF],
                 )
             x_codes[t], x_scales[t] = codes, scales
 
         def project(m, c, t, half):
-            col = half * ROT + c * N
             acc = psum.tile([P, N], F32, name="bank")
             for g in range(PASSES):
                 tokens = slice(g * P, (g + 1) * P)
@@ -146,8 +146,8 @@ def tile_attention_pa_kernel(tc, x, cos, sin, Wq_words, Wq_scales, Wk_words, Wk_
                     out=acc[:],
                     lhsT=x_codes[t][:, tokens].bitcast(E5M2X4),
                     lhsT_scale=x_scales[t][:, tokens],
-                    rhs=w_words[m, col][:, g, :].bitcast(E2M1X4),
-                    rhs_scale=w_scales[m, col][:, g, :],
+                    rhs=w_words[m, c, half][:, g, :].bitcast(E2M1X4),
+                    rhs_scale=w_scales[m, c, half][:, g, :],
                     start=(g == 0),
                     stop=(g == PASSES - 1),
                 )
@@ -163,87 +163,89 @@ def tile_attention_pa_kernel(tc, x, cos, sin, Wq_words, Wq_scales, Wk_words, Wk_
                 op=MULT,
             )
 
-        def subtract(m, c, t):
-            if m == Q and t < WHOLE_ROW_TILES:
+        def subtract_and_store(m, c, t):
+            rows = outs[m][0, t * P:(t + 1) * P, :]
+            prod = prods[m, c, t]
+            cos_terms, sin_terms = prod[:, COS_LOW:COS_HIGH + 1, :], prod[:, SIN_LOW:SIN_HIGH + 1, :]
+            if m == Q:
                 if c == 0:
                     results[Q, t] = keep.tile([P, D], F32, name=f"q_rows_{t}", align_bytes=64)
-                dest = paired(results[Q, t][:], c)
-            else:
-                results[m, c, t] = keep.tile([P, 2, N], F32, name=f"block_{m}_{c}_{t}", align_bytes=64)
-                dest = results[m, c, t][:]
-            prod = prods[m, c, t]
-            nc.gpsimd.tensor_tensor(out=dest, in0=prod[:, 0:2, :], in1=prod[:, 2:4, :], op=SUB)
-
-        def store(m, c, t):
-            rows = outs[m][0, t * P:(t + 1) * P, :]
-            if m == Q and t < WHOLE_ROW_TILES:
-                if c == 1:
+                nc.gpsimd.tensor_tensor(out=paired(results[Q, t][:], c), in0=cos_terms, in1=sin_terms, op=SUB)
+                if c == BLOCKS - 1:
                     nc.sync.dma_start(out=rows, in_=results[Q, t][:])
             else:
-                nc.sync.dma_start(out=paired(rows, c), in_=results[m, c, t][:])
+                block = keep.tile([P, 2, N], F32, name=f"k_block_{c}_{t}", align_bytes=64)
+                nc.gpsimd.tensor_tensor(out=block[:], in0=cos_terms, in1=sin_terms, op=SUB)
+                nc.sync.dma_start(out=paired(rows, c), in_=block[:])
 
         def subtract_half_and_store(engine, m, c, t, half):
-            rows = paired(outs[m][0, t * P:(t + 1) * P, :], c)
-            prod = prods[m, c, t]
-            engine.tensor_tensor(out=prod[:, half, :], in0=prod[:, half, :], in1=prod[:, 2 + half, :], op=SUB)
-            nc.sync.dma_start(out=rows[:, half, :], in_=prod[:, half, :])
+            rows = outs[m][0, t * P:(t + 1) * P, :]
+            cos_term = prods[m, c, t][:, COS_LOW + half, :]
+            engine.tensor_tensor(out=cos_term, in0=cos_term, in1=prods[m, c, t][:, SIN_LOW + half, :], op=SUB)
+            nc.sync.dma_start(out=paired(rows, c)[:, half, :], in_=cos_term)
 
         ident = keep.tile([P, P], F32, name="ident", align_bytes=64)
         make_identity(nc, ident[:])
-        for c in range(2):
+        for c in range(BLOCKS):
             for m in (Q, K):
                 for half in (HIGH, LOW):
-                    zero_plane(m, half * ROT + c * N)
+                    zero_scales(m, c, half)
 
         load_x(0, 2)
         load_x(1, 1)
-        load_x(2, 1)
-        for c in range(2):
-            load_words(Q, c, HIGH)
-            if c == 0:
-                load_x(3, 1)
-            load_table_part(0, c, COS_HIGH)
-            load_table_part(0, c, SIN_LOW)
-            load_words(Q, c, LOW)
-            load_table_part(0, c, SIN_HIGH)
-            load_table_part(0, c, COS_LOW)
-            for part in (SIN_HIGH, COS_HIGH, SIN_LOW, COS_LOW):
-                load_table_part(2, c, part)
-            load_words(K, c, HIGH)
-            load_words(K, c, LOW)
+        load_weights(Q, 0, HIGH)
+        for t in range(2, TILES):
+            load_x(t, 1)
+        for part in (COS_HIGH, SIN_LOW):
+            load_table_parts(0, 0, part, part)
+        load_weights(Q, 0, LOW)
+        for part in (SIN_HIGH, COS_LOW):
+            load_table_parts(0, 0, part, part)
+        for t in range(1, TILES):
+            load_tables(t, 0)
+        for half in (HIGH, LOW):
+            load_weights(K, 0, half)
+        for c in range(1, BLOCKS):
+            for half in (HIGH, LOW):
+                load_weights(Q, c, half)
+            for t in range(TILES):
+                load_tables(t, c)
+            for half in (HIGH, LOW):
+                load_weights(K, c, half)
 
-        order_words(0, None)
-        order_words(1, nc.vector.tensor_copy)
-        order_words(2, nc.vector.tensor_copy)
+        for t in range(2):
+            order_words(t)
         for t in range(2):
             transpose_tokens(t)
-            quantize_tokens(t, 2)
-        transpose_tokens(2)
-        order_words(3, nc.vector.tensor_copy)
-        quantize_tokens(2, 2)
+            quantize_tokens(t)
+        project(Q, 0, 0, HIGH)
+        for t in range(2, TILES):
+            order_words(t)
+            transpose_tokens(t)
+        project(Q, 0, 1, HIGH)
+        multiply(Q, 0, 0, HIGH)
+        for t in range(2, TILES):
+            quantize_tokens(t)
 
-        steps = [(m, c, t) for c in range(2) for m in (Q, K) for t in range(TILES)]
-        by_halves = steps[-LAST_STEPS:]
-        banks = []
-        for c in range(2):
-            for m in (Q, K):
-                if c == 0:
-                    banks += [(m, c, t, half) for half in (HIGH, LOW) for t in range(2)]
-                    banks += [(m, c, t, half) for t in range(2, TILES) for half in (HIGH, LOW)]
-                else:
-                    banks += [(m, c, t, half) for t in range(TILES) for half in (HIGH, LOW)]
-        for m, c, t, half in banks:
-            if (m, c, t, half) == (Q, 0, 1, HIGH):
-                transpose_tokens(3)
-                quantize_tokens(3, 2)
-            if m == Q and half == LOW and t % 2 == 0:
+        steps = [(m, c, t) for c in range(BLOCKS) for m in (Q, K) for t in range(TILES)]
+        bank_order = []
+        for m, c, t in steps:
+            if (m, c) == (K, 0) and t < 2:
+                half = (HIGH, LOW)[t]
+                bank_order += [(m, c, 0, half), (m, c, 1, half)]
+            else:
+                bank_order += [(m, c, t, HIGH), (m, c, t, LOW)]
+        last_steps = steps[-LAST_STEPS:]
+        for m, c, t, half in bank_order[1:]:
+            if m == Q and half == LOW:
                 negate_sin_high(t, c)
-            project(m, c, t, half)
+            if (m, c, t, half) not in accs:
+                project(m, c, t, half)
             multiply(m, c, t, half)
-            if half == LOW and (m, c, t) not in by_halves:
-                subtract(m, c, t)
-                store(m, c, t)
-        last_halves = [(*step, half) for step in by_halves for half in (LOW, HIGH)]
+            if half == LOW and (m, c, t) not in last_steps:
+                subtract_and_store(m, c, t)
+
+        last_halves = [(m, c, t, half) for m, c, t in last_steps for half in (LOW, HIGH)]
         subtract_half_and_store(nc.gpsimd, *last_halves[0])
         for piece in last_halves[1:]:
             subtract_half_and_store(nc.vector, *piece)

from contextlib import ExitStack

import concourse.mybir as mybir
from concourse.masks import make_identity

S, D = 512, 2048
FLOPS = 2 * 2 * S * D * D

F32 = mybir.dt.float32
BF16 = mybir.dt.bfloat16
I32 = mybir.dt.int32
U32 = mybir.dt.uint32
U8 = mybir.dt.uint8
E5M2X4 = mybir.dt.float8_e5m2_x4
E2M1X4 = mybir.dt.float4_e2m1fn_x4
MULT = mybir.AluOpType.mult
SUB = mybir.AluOpType.subtract

P = 128
PACK = 4
PASSES = D // (P * PACK)
K_HALF = D // 2
N = 512
ROT = D // 2
BLOCKS = ROT // N
TILES = S // P
Q, K = 0, 1
LOW, HIGH = 0, 1

COS_LOW, COS_HIGH, SIN_LOW, SIN_HIGH = 0, 1, 2, 3
PARTS = {HIGH: slice(COS_HIGH, SIN_LOW + 1), LOW: slice(COS_LOW, SIN_HIGH + 1, SIN_HIGH - COS_LOW)}

LAST_STEPS = 3
PRODUCT_BUFS = 5


def tile_attention_pa_kernel(tc, x, cos, sin, Wq_words, Wq_scales, Wk_words, Wk_scales, out_0, out_1):
    nc = tc.nc
    w_words_hbm = (Wq_words, Wk_words)
    w_scales_hbm = (Wq_scales, Wk_scales)
    outs = (out_0, out_1)

    with ExitStack() as ctx:
        keep = ctx.enter_context(tc.tile_pool(name="keep", bufs=1))
        stage = ctx.enter_context(tc.tile_pool(name="stage", bufs=2))
        products = ctx.enter_context(tc.tile_pool(name="products", bufs=PRODUCT_BUFS))
        psum = ctx.enter_context(tc.psum_pool(name="psum", bufs=8))
        ctx.enter_context(tc.manual_schedule())

        x_raw, x_words, x_grouped, x_codes, x_scales = {}, {}, {}, {}, {}
        w_words, w_scales, tables = {}, {}, {}
        accs, prods, results = {}, {}, {}

        def paired(rows, c):
            return rows.rearrange("p (half n) -> p half n", half=2)[:, :, c * N:(c + 1) * N]

        def zero_scales(m, c, half):
            scales = keep.tile([P, PASSES, N], U8, name=f"w_scales_{m}_{c}_{half}", align_bytes=64)
            nc.vector.memset(scales[:].rearrange("p g n -> p (g n)").bitcast(I32), 0)
            w_scales[m, c, half] = scales

        def load_weights(m, c, half):
            col = half * ROT + c * N
            for r in range(4):
                nc.sync.dma_start(
                    out=w_scales[m, c, half][r:P:32, :, :].bitcast(I32),
                    in_=w_scales_hbm[m][:, r:16:4, col:col + N].rearrange("g q n -> q g n").bitcast(I32),
                )
            words = keep.tile([P, PASSES, 2 * N], U8, name=f"w_words_{m}_{c}_{half}", align_bytes=64)
            nc.sync.dma_start(
                out=words[:].bitcast(I32),
                in_=w_words_hbm[m][:, :, 2 * col:2 * (col + N)].rearrange("g p n -> p g n").bitcast(I32),
            )
            w_words[m, c, half] = words

        def load_x(t, pieces):
            raw = keep.tile([P, D], BF16, name=f"x_{t}", align_bytes=64)
            for k0 in range(0, D, D // pieces):
                k_cols = slice(k0, k0 + D // pieces)
                nc.sync.dma_start(out=raw[:, k_cols], in_=x[0, t * P:(t + 1) * P, k_cols])
            x_raw[t] = raw

        def load_table_parts(t, c, first, last):
            if (t, c) not in tables:
                tables[t, c] = keep.tile([P, 4, N], BF16, name=f"tables_{t}_{c}", align_bytes=64)
            table = cos if first in (COS_LOW, COS_HIGH) else sin
            halves = paired(table[t * P:(t + 1) * P, :], c)
            nc.sync.dma_start(out=tables[t, c][:, first:last + 1, :], in_=halves[:, first % 2:last % 2 + 1, :])

        def load_tables(t, c):
            load_table_parts(t, c, SIN_LOW, SIN_HIGH)
            load_table_parts(t, c, COS_LOW, COS_HIGH)

        def negate_sin_high(t, c):
            part = tables[t, c][:, SIN_HIGH, :]
            if (t, c) == (0, 0):
                nc.vector.tensor_scalar_mul(part, part, -1.0)
            else:
                nc.scalar.mul(out=part, in_=part, mul=-1.0)

        def order_words(t):
            for kh in range(2):
                words = x_raw[t][:, kh * K_HALF:(kh + 1) * K_HALF].bitcast(F32)
                words = words.rearrange("p (g i u) -> p g u i", g=2, u=2)
                if t == 0:
                    x_words[t, kh] = words
                else:
                    ordered = stage.tile([P, 2, 2, P], F32, name="ordered", align_bytes=64, bufs=4)
                    nc.vector.tensor_copy(out=ordered[:], in_=words)
                    x_words[t, kh] = ordered

        def transpose_tokens(t):
            grouped = stage.tile([P, D], BF16, name="grouped", align_bytes=64)
            banks = {}
            for kh in range(2):
                bank = psum.tile([P, 2, 2, P], F32, name="bank")
                for g in range(2):
                    for u in range(2):
                        nc.tensor.transpose(bank[:, g, u, :], x_words[t, kh][:, g, u, :], ident[:])
                banks[kh] = bank
            for kh in range(2):
                half_of_k = grouped[:, kh * K_HALF:(kh + 1) * K_HALF].bitcast(F32)
                nc.scalar.copy(
                    out=half_of_k.rearrange("p (g r u) -> p g r u", g=2, u=2),
                    in_=banks[kh][:].rearrange("p g u r -> p g r u"),
                )
            x_grouped[t] = grouped

        def quantize_tokens(t):
            codes = keep.tile([P, PASSES * P], U32, name=f"x_codes_{t}", align_bytes=64)
            scales = keep.tile([P, PASSES * P], U8, name=f"x_scales_{t}", align_bytes=64)
            for kh in range(2):
                cols = slice(kh * K_HALF // PACK, (kh + 1) * K_HALF // PACK)
                nc.vector.quantize_mx(
                    out=codes[:, cols].bitcast(E5M2X4),
                    scales=scales[:, cols],
                    in_=x_grouped[t][:, kh * K_HALF:(kh + 1) * K_HALF],
                )
            x_codes[t], x_scales[t] = codes, scales

        def project(m, c, t, half):
            acc = psum.tile([P, N], F32, name="bank")
            for g in range(PASSES):
                tokens = slice(g * P, (g + 1) * P)
                nc.tensor.matmul_mx(
                    out=acc[:],
                    lhsT=x_codes[t][:, tokens].bitcast(E5M2X4),
                    lhsT_scale=x_scales[t][:, tokens],
                    rhs=w_words[m, c, half][:, g, :].bitcast(E2M1X4),
                    rhs_scale=w_scales[m, c, half][:, g, :],
                    start=(g == 0),
                    stop=(g == PASSES - 1),
                )
            accs[m, c, t, half] = acc

        def multiply(m, c, t, half):
            if half == HIGH:
                prods[m, c, t] = products.tile([P, 4, N], F32, name="prod", align_bytes=64)
            nc.vector.tensor_tensor(
                out=prods[m, c, t][:, PARTS[half], :],
                in0=accs[m, c, t, half][:].unsqueeze(1).to_broadcast([P, 2, N]),
                in1=tables[t, c][:, PARTS[half], :],
                op=MULT,
            )

        def subtract_and_store(m, c, t):
            rows = outs[m][0, t * P:(t + 1) * P, :]
            prod = prods[m, c, t]
            cos_terms, sin_terms = prod[:, COS_LOW:COS_HIGH + 1, :], prod[:, SIN_LOW:SIN_HIGH + 1, :]
            if m == Q:
                if c == 0:
                    results[Q, t] = keep.tile([P, D], F32, name=f"q_rows_{t}", align_bytes=64)
                nc.gpsimd.tensor_tensor(out=paired(results[Q, t][:], c), in0=cos_terms, in1=sin_terms, op=SUB)
                if c == BLOCKS - 1:
                    nc.sync.dma_start(out=rows, in_=results[Q, t][:])
            else:
                block = keep.tile([P, 2, N], F32, name=f"k_block_{c}_{t}", align_bytes=64)
                nc.gpsimd.tensor_tensor(out=block[:], in0=cos_terms, in1=sin_terms, op=SUB)
                nc.sync.dma_start(out=paired(rows, c), in_=block[:])

        def subtract_half_and_store(engine, m, c, t, half):
            rows = outs[m][0, t * P:(t + 1) * P, :]
            cos_term = prods[m, c, t][:, COS_LOW + half, :]
            engine.tensor_tensor(out=cos_term, in0=cos_term, in1=prods[m, c, t][:, SIN_LOW + half, :], op=SUB)
            nc.sync.dma_start(out=paired(rows, c)[:, half, :], in_=cos_term)

        ident = keep.tile([P, P], F32, name="ident", align_bytes=64)
        make_identity(nc, ident[:])
        for c in range(BLOCKS):
            for m in (Q, K):
                for half in (HIGH, LOW):
                    zero_scales(m, c, half)

        load_x(0, 2)
        load_x(1, 1)
        load_weights(Q, 0, HIGH)
        for t in range(2, TILES):
            load_x(t, 1)
        for part in (COS_HIGH, SIN_LOW):
            load_table_parts(0, 0, part, part)
        load_weights(Q, 0, LOW)
        for part in (SIN_HIGH, COS_LOW):
            load_table_parts(0, 0, part, part)
        for t in range(1, TILES):
            load_tables(t, 0)
        for half in (HIGH, LOW):
            load_weights(K, 0, half)
        for c in range(1, BLOCKS):
            for half in (HIGH, LOW):
                load_weights(Q, c, half)
            for t in range(TILES):
                load_tables(t, c)
            for half in (HIGH, LOW):
                load_weights(K, c, half)

        for t in range(2):
            order_words(t)
        for t in range(2):
            transpose_tokens(t)
            quantize_tokens(t)
        project(Q, 0, 0, HIGH)
        for t in range(2, TILES):
            order_words(t)
            transpose_tokens(t)
        project(Q, 0, 1, HIGH)
        multiply(Q, 0, 0, HIGH)
        for t in range(2, TILES):
            quantize_tokens(t)

        steps = [(m, c, t) for c in range(BLOCKS) for m in (Q, K) for t in range(TILES)]
        bank_order = []
        for m, c, t in steps:
            if (m, c) == (K, 0) and t < 2:
                half = (HIGH, LOW)[t]
                bank_order += [(m, c, 0, half), (m, c, 1, half)]
            else:
                bank_order += [(m, c, t, HIGH), (m, c, t, LOW)]
        last_steps = steps[-LAST_STEPS:]
        for m, c, t, half in bank_order[1:]:
            if m == Q and half == LOW:
                negate_sin_high(t, c)
            if (m, c, t, half) not in accs:
                project(m, c, t, half)
            multiply(m, c, t, half)
            if half == LOW and (m, c, t) not in last_steps:
                subtract_and_store(m, c, t)

        last_halves = [(m, c, t, half) for m, c, t in last_steps for half in (LOW, HIGH)]
        subtract_half_and_store(nc.gpsimd, *last_halves[0])
        for piece in last_halves[1:]:
            subtract_half_and_store(nc.vector, *piece)
